import numpy as np
import ml_dtypes


def mxq(x, axis, fmt="e4m3"):
    dtype, down = {"e4m3": (ml_dtypes.float8_e4m3fn, 7), "e5m2": (ml_dtypes.float8_e5m2, 14)}[fmt]
    v = np.moveaxis(np.asarray(x, np.float32).astype(ml_dtypes.bfloat16).astype(np.float64), axis, -1)
    blocks = v.reshape(v.shape[:-1] + (-1, 32))
    amax = np.abs(blocks).max(-1, keepdims=True)
    byte = np.maximum(np.where(amax > 0, np.frexp(amax)[1] - 1 + 127, 0) - down, 1)
    scale = np.exp2(byte - 127.0)
    codes = (blocks / scale).astype(np.float32).astype(dtype).astype(np.float64)
    return np.moveaxis((codes * scale).reshape(v.shape), -1, axis)


WIDE = False


def mx_kscale(k):
    if not WIDE:
        return np.ones(k)
    levels = np.array([20, -20, 10, -10, 0])
    a = np.random.permutation(np.resize(levels, k // 512 * 4)).reshape(k // 512, 4)
    idx = np.arange(k)
    return np.exp2(a[idx // 512, idx % 128 // 32])


BF16 = ml_dtypes.bfloat16


def bf(x):
    return np.asarray(x, np.float32).astype(BF16)


def f64(x):
    return np.asarray(x).astype(np.float64)


BS, CIN, COUT, OUT_DIM, BLK = 1024, 128, 512, 8, 4
D = OUT_DIM * BLK


def setup_inputs():
    u = mx_kscale(COUT)
    x = np.random.standard_normal((BS, CIN, D))
    weight = np.random.standard_normal((COUT, CIN, D)) / u[:, None, None]
    g = np.random.standard_normal((BS, COUT, OUT_DIM)) * np.exp2(np.random.randint(-12, 1, (BS, 1, OUT_DIM))) * u[None, :, None]
    return {"x": bf(x), "weight": bf(weight), "grad_out": bf(g)}


def reference(x, weight, grad_out):
    cout, cin, d = weight.shape
    bs = grad_out.shape[0]
    n = d // BLK
    g = f64(grad_out).transpose(2, 0, 1)
    wr = f64(weight).reshape(cout, cin, n, BLK).transpose(2, 0, 1, 3).reshape(n, cout, cin * BLK)
    gx = mxq(g, 2, "e5m2") @ mxq(wr, 1, "e4m3")
    return gx.reshape(n, bs, cin, BLK).transpose(1, 2, 0, 3).reshape(bs, cin, d) / np.sqrt(cin)

@@ -1,0 +1,151 @@
+import math
+from contextlib import ExitStack
+
+import concourse.mybir as mybir
+from concourse.masks import make_identity
+
+BF16 = mybir.dt.bfloat16
+F32 = mybir.dt.float32
+U32 = mybir.dt.uint32
+U8 = mybir.dt.uint8
+E4M3X4 = mybir.dt.float8_e4m3fn_x4
+E5M2X4 = mybir.dt.float8_e5m2_x4
+
+P = 128
+BS, CIN, COUT, NPOS, BLK = 1024, 128, 512, 8, 4
+D = NPOS * BLK
+PACK = 4
+NBT = BS // P
+COLS = CIN * BLK
+WCH = 4
+IC = CIN // WCH
+SCALE = 1.0 / math.sqrt(CIN)
+
+FLOPS = 2 * NPOS * BS * COUT * COLS
+BYTES = 2 * COUT * CIN * D + 2 * BS * COUT * NPOS + 4 * BS * CIN * D
+
+V_NPOS = 6
+
+
+def tile_nonoverlappinglocallyconnected1d_t_kernel(tc, x, weight, grad_out, out):
+    nc = tc.nc
+    gv = grad_out.rearrange("(j p) o n -> j p (o n)", p=P)
+    ov = out.rearrange("(j p) i d -> j p (i d)", p=P)
+    wv = weight.rearrange("(t p) i d -> p t (i d)", p=P)
+
+    with ExitStack() as ctx:
+        const = ctx.enter_context(tc.tile_pool(name="const", bufs=1))
+        gpool = ctx.enter_context(tc.tile_pool(name="gpool", bufs=6))
+        wraw_pool = ctx.enter_context(tc.tile_pool(name="wraw", bufs=WCH))
+        grp_pool = ctx.enter_context(tc.tile_pool(name="grp", bufs=2))
+        code_pool = ctx.enter_context(tc.tile_pool(name="code", bufs=2))
+        opool = ctx.enter_context(tc.tile_pool(name="opool", bufs=4))
+        xt_pool = ctx.enter_context(tc.psum_pool(name="xt", bufs=4))
+        acc_pool = ctx.enter_context(tc.psum_pool(name="acc", bufs=4))
+
+        ident = const.tile([P, P], F32)
+        make_identity(nc, ident[:])
+        wg = const.tile([P, NPOS * COLS * PACK], BF16, align_bytes=64)
+        wc = const.tile([P, NPOS * COLS], U32, align_bytes=64)
+        ws = const.tile([P, NPOS * COLS], U8, align_bytes=64)
+
+        g_sb = {}
+        xts = {}
+        grouped = {}
+        g_codes = {}
+        g_scales = {}
+        w_raw = {}
+
+        def load_g(j):
+            g_sb[j] = gpool.tile([P, COUT * NPOS], BF16, name="g_sb")
+            nc.sync.dma_start(out=g_sb[j][:], in_=gv[j])
+
+        def load_w(c):
+            w_raw[c] = wraw_pool.tile([P, PACK, IC * D], BF16, name="w_raw")
+            nc.sync.dma_start(out=w_raw[c][:], in_=wv[:, :, c * IC * D : (c + 1) * IC * D])
+
+        def transposes(j):
+            words = g_sb[j][:].bitcast(F32).rearrange("p (o m) -> p o m", m=NPOS // 2)
+            for m in range(NPOS // 2):
+                xts[(j, m)] = xt_pool.tile([P, PACK * P], F32, name="xt")
+                for t in range(PACK):
+                    nc.tensor.transpose(
+                        xts[(j, m)][:, t * P : (t + 1) * P], words[:, t * P : (t + 1) * P, m], ident[:]
+                    )
+
+        def copies(j):
+            grouped[j] = grp_pool.tile([P, NPOS * P * PACK], BF16, name="grouped", align_bytes=64)
+            for m in range(NPOS // 2):
+                dst = grouped[j][:, m * 2 * P * PACK : (m + 1) * 2 * P * PACK].rearrange(
+                    "p (e b t) -> p e b t", e=2, t=PACK
+                )
+                src = xts[(j, m)][:].bitcast(BF16).rearrange("p (t b e) -> p e b t", t=PACK, e=2)
+                if m == 3 or (m == 1 and j % 2 == 0):
+                    nc.vector.tensor_copy(out=dst, in_=src)
+                else:
+                    nc.scalar.copy(out=dst, in_=src)
+
+        def quantise_g(j):
+            g_codes[j] = code_pool.tile([P, NPOS * P], U32, name="g_codes", align_bytes=64)
+            g_scales[j] = code_pool.tile([P, NPOS * P], U8, name="g_scales", align_bytes=64)
+            nc.vector.quantize_mx(out=g_codes[j][:].bitcast(E5M2X4), scales=g_scales[j][:], in_=grouped[j][:])
+
+        def regroup_w(c):
+            src = w_raw[c][:].rearrange("p t (i n k) -> p n i t k", n=NPOS, k=BLK)
+            dst = wg[:].rearrange("p (n i k t) -> p n i t k", n=NPOS, k=BLK, t=PACK)[:, :, c * IC : (c + 1) * IC]
+            nc.vector.tensor_copy(out=dst[:, 0:V_NPOS], in_=src[:, 0:V_NPOS])
+            for n in range(V_NPOS, NPOS):
+                nc.scalar.copy(out=dst[:, n], in_=src[:, n])
+
+        def quantise_w(n):
+            nc.vector.quantize_mx(
+                out=wc[:, n * COLS : (n + 1) * COLS].bitcast(E4M3X4),
+                scales=ws[:, n * COLS : (n + 1) * COLS],
+                in_=wg[:, n * COLS * PACK : (n + 1) * COLS * PACK],
+            )
+
+        def product(j, n, o_sb):
+            acc = acc_pool.tile([P, COLS], F32, name="acc")
+            nc.tensor.matmul_mx(
+                out=acc[:],
+                lhsT=g_codes[j][:, n * P : (n + 1) * P].bitcast(E5M2X4),
+                lhsT_scale=g_scales[j][:, n * P : (n + 1) * P],
+                rhs=wc[:, n * COLS : (n + 1) * COLS].bitcast(E4M3X4),
+                rhs_scale=ws[:, n * COLS : (n + 1) * COLS],
+                start=True,
+                stop=True,
+            )
+            dst = o_sb[:].rearrange("p (i n k) -> p n i k", n=NPOS, k=BLK)[:, n]
+            src = acc[:].rearrange("p (i k) -> p i k", k=BLK)
+            on_scalar = (n < 6) if j == 0 else (n >= 4)
+            if on_scalar:
+                nc.scalar.mul(out=dst, in_=src, mul=SCALE)
+            else:
+                nc.vector.tensor_scalar(out=dst, in0=src, scalar1=SCALE, scalar2=None, op0=mybir.AluOpType.mult)
+
+        load_g(0)
+        for c in range(WCH):
+            load_w(c)
+        for j in range(1, 6):
+            load_g(j)
+        transposes(0)
+        copies(0)
+        for c in range(WCH):
+            regroup_w(c)
+        quantise_g(0)
+        transposes(1)
+        for j in range(6, NBT):
+            load_g(j)
+        copies(1)
+        for j in range(NBT):
+            o_sb = opool.tile([P, CIN * D], F32, name="o_sb")
+            for n in range(NPOS):
+                if j == 0:
+                    quantise_w(n)
+                product(j, n, o_sb)
+            nc.sync.dma_start(out=ov[j], in_=o_sb[:])
+            if j + 1 < NBT:
+                quantise_g(j + 1)
+            if j + 2 < NBT:
+                transposes(j + 2)
+                copies(j + 2)

@@ -35,7 +35,8 @@ def tile_nonoverlappinglocallyconnected1d_t_kernel(tc, x, weight, grad_out, out)
 
     with ExitStack() as ctx:
         const = ctx.enter_context(tc.tile_pool(name="const", bufs=1))
-        gpool = ctx.enter_context(tc.tile_pool(name="gpool", bufs=6))
+        gpool = ctx.enter_context(tc.tile_pool(name="gpool", bufs=5))
+        spool = ctx.enter_context(tc.tile_pool(name="spool", bufs=3))
         wraw_pool = ctx.enter_context(tc.tile_pool(name="wraw", bufs=WCH))
         grp_pool = ctx.enter_context(tc.tile_pool(name="grp", bufs=2))
         code_pool = ctx.enter_context(tc.tile_pool(name="code", bufs=2))
@@ -50,6 +51,7 @@ def tile_nonoverlappinglocallyconnected1d_t_kernel(tc, x, weight, grad_out, out)
         ws = const.tile([P, NPOS * COLS], U8, align_bytes=64)
 
         g_sb = {}
+        g_sorted = {}
         xts = {}
         grouped = {}
         g_codes = {}
@@ -64,23 +66,46 @@ def tile_nonoverlappinglocallyconnected1d_t_kernel(tc, x, weight, grad_out, out)
             w_raw[c] = wraw_pool.tile([P, PACK, IC * D], BF16, name="w_raw")
             nc.sync.dma_start(out=w_raw[c][:], in_=wv[:, :, c * IC * D : (c + 1) * IC * D])
 
+        def sort_g(j):
+            g_sorted[j] = spool.tile([P, COUT * NPOS // 2], BF16, name="g_sorted")
+            src = g_sb[j][:].rearrange("b (u e q n) -> b u n q e", u=2, e=2, n=NPOS)
+            dst = g_sorted[j][:].rearrange("b (n u q e) -> b u n q e", u=2, e=2, n=NPOS // 2)
+            for u in range(2):
+                nc.gpsimd.tensor_scalar(
+                    out=dst[:, u],
+                    in0=src[:, u, NPOS // 2 : NPOS],
+                    scalar1=1.0,
+                    scalar2=0.0,
+                    op0=mybir.AluOpType.mult,
+                    op1=mybir.AluOpType.add,
+                )
+
         def transposes(j):
             words = g_sb[j][:].bitcast(F32).rearrange("p (o m) -> p o m", m=NPOS // 2)
+            sorted_words = g_sorted[j][:].bitcast(F32)
             for m in range(NPOS // 2):
                 xts[(j, m)] = xt_pool.tile([P, PACK * P], F32, name="xt")
                 for t in range(PACK):
-                    nc.tensor.transpose(
-                        xts[(j, m)][:, t * P : (t + 1) * P], words[:, t * P : (t + 1) * P, m], ident[:]
-                    )
+                    if m < 2:
+                        in_ = words[:, t * P : (t + 1) * P, m]
+                    else:
+                        in_ = sorted_words[:, ((m - 2) * PACK + t) * P : ((m - 2) * PACK + t + 1) * P]
+                    nc.tensor.transpose(xts[(j, m)][:, t * P : (t + 1) * P], in_, ident[:])
 
         def copies(j):
             grouped[j] = grp_pool.tile([P, NPOS * P * PACK], BF16, name="grouped", align_bytes=64)
             for m in range(NPOS // 2):
-                dst = grouped[j][:, m * 2 * P * PACK : (m + 1) * 2 * P * PACK].rearrange(
-                    "p (e b t) -> p e b t", e=2, t=PACK
-                )
-                src = xts[(j, m)][:].bitcast(BF16).rearrange("p (t b e) -> p e b t", t=PACK, e=2)
-                if m == 3 or (m == 1 and j % 2 == 0):
+                if m < 2:
+                    dst = grouped[j][:, m * 2 * P * PACK : (m + 1) * 2 * P * PACK].rearrange(
+                        "p (e b t) -> p e b t", e=2, t=PACK
+                    )
+                    src = xts[(j, m)][:].bitcast(BF16).rearrange("p (t b e) -> p e b t", t=PACK, e=2)
+                else:
+                    dst = grouped[j][:].bitcast(F32)[:, m * P * PACK : (m + 1) * P * PACK].rearrange(
+                        "p (n b u) -> p n b u", n=2, u=2
+                    )
+                    src = xts[(j, m)][:].rearrange("p (n u b) -> p n b u", n=2, u=2)
+                if m == 3:
                     nc.vector.tensor_copy(out=dst, in_=src)
                 else:
                     nc.scalar.copy(out=dst, in_=src)
@@ -117,7 +142,7 @@ def tile_nonoverlappinglocallyconnected1d_t_kernel(tc, x, weight, grad_out, out)
             )
             dst = o_sb[:].rearrange("p (i n k) -> p n i k", n=NPOS, k=BLK)[:, n]
             src = acc[:].rearrange("p (i k) -> p i k", k=BLK)
-            on_scalar = (n < 6) if j == 0 else (n >= 4)
+            on_scalar = n >= 4
             if on_scalar:
                 nc.scalar.mul(out=dst, in_=src, mul=SCALE)
             else:
@@ -126,18 +151,25 @@ def tile_nonoverlappinglocallyconnected1d_t_kernel(tc, x, weight, grad_out, out)
         load_g(0)
         for c in range(WCH):
             load_w(c)
-        for j in range(1, 6):
+        for j in range(1, 5):
             load_g(j)
+        sort_g(0)
         transposes(0)
         copies(0)
+        load_g(5)
         for c in range(WCH):
             regroup_w(c)
         quantise_g(0)
+        sort_g(1)
         transposes(1)
-        for j in range(6, NBT):
-            load_g(j)
         copies(1)
+        load_g(6)
         for j in range(NBT):
+            if j + 2 < NBT:
+                sort_g(j + 2)
+                transposes(j + 2)
+            if j == 0:
+                load_g(7)
             o_sb = opool.tile([P, CIN * D], F32, name="o_sb")
             for n in range(NPOS):
                 if j == 0:
@@ -147,5 +179,4 @@ def tile_nonoverlappinglocallyconnected1d_t_kernel(tc, x, weight, grad_out, out)
             if j + 1 < NBT:
                 quantise_g(j + 1)
             if j + 2 < NBT:
-                transposes(j + 2)
                 copies(j + 2)

@@ -16,15 +16,19 @@ BS, CIN, COUT, NPOS, BLK = 1024, 128, 512, 8, 4
 D = NPOS * BLK
 PACK = 4
 NBT = BS // P
+NPAIR = NPOS // 2
 COLS = CIN * BLK
 WCH = 4
 IC = CIN // WCH
+G_BUFS = 6
 SCALE = 1.0 / math.sqrt(CIN)
 
 FLOPS = 2 * NPOS * BS * COUT * COLS
 BYTES = 2 * COUT * CIN * D + 2 * BS * COUT * NPOS + 4 * BS * CIN * D
 
 V_NPOS = 6
+V_SECOND_BANK = (0, 4, 6)
+LAST = NBT - 1
 
 
 def tile_nonoverlappinglocallyconnected1d_t_kernel(tc, x, weight, grad_out, out):
@@ -35,14 +39,13 @@ def tile_nonoverlappinglocallyconnected1d_t_kernel(tc, x, weight, grad_out, out)
 
     with ExitStack() as ctx:
         const = ctx.enter_context(tc.tile_pool(name="const", bufs=1))
-        gpool = ctx.enter_context(tc.tile_pool(name="gpool", bufs=5))
-        spool = ctx.enter_context(tc.tile_pool(name="spool", bufs=3))
+        gpool = ctx.enter_context(tc.tile_pool(name="gpool", bufs=G_BUFS))
         wraw_pool = ctx.enter_context(tc.tile_pool(name="wraw", bufs=WCH))
         grp_pool = ctx.enter_context(tc.tile_pool(name="grp", bufs=2))
         code_pool = ctx.enter_context(tc.tile_pool(name="code", bufs=2))
         opool = ctx.enter_context(tc.tile_pool(name="opool", bufs=4))
-        xt_pool = ctx.enter_context(tc.psum_pool(name="xt", bufs=4))
-        acc_pool = ctx.enter_context(tc.psum_pool(name="acc", bufs=4))
+        psum = ctx.enter_context(tc.psum_pool(name="psum", bufs=1))
+        ctx.enter_context(tc.manual_schedule())
 
         ident = const.tile([P, P], F32)
         make_identity(nc, ident[:])
@@ -51,12 +54,13 @@ def tile_nonoverlappinglocallyconnected1d_t_kernel(tc, x, weight, grad_out, out)
         ws = const.tile([P, NPOS * COLS], U8, align_bytes=64)
 
         g_sb = {}
-        g_sorted = {}
         xts = {}
         grouped = {}
         g_codes = {}
         g_scales = {}
         w_raw = {}
+        accs = {}
+        o_sb = {}
 
         def load_g(j):
             g_sb[j] = gpool.tile([P, COUT * NPOS], BF16, name="g_sb")
@@ -66,49 +70,23 @@ def tile_nonoverlappinglocallyconnected1d_t_kernel(tc, x, weight, grad_out, out)
             w_raw[c] = wraw_pool.tile([P, PACK, IC * D], BF16, name="w_raw")
             nc.sync.dma_start(out=w_raw[c][:], in_=wv[:, :, c * IC * D : (c + 1) * IC * D])
 
-        def sort_g(j):
-            g_sorted[j] = spool.tile([P, COUT * NPOS // 2], BF16, name="g_sorted")
-            src = g_sb[j][:].rearrange("b (u e q n) -> b u n q e", u=2, e=2, n=NPOS)
-            dst = g_sorted[j][:].rearrange("b (n u q e) -> b u n q e", u=2, e=2, n=NPOS // 2)
-            for u in range(2):
-                nc.gpsimd.tensor_scalar(
-                    out=dst[:, u],
-                    in0=src[:, u, NPOS // 2 : NPOS],
-                    scalar1=1.0,
-                    scalar2=0.0,
-                    op0=mybir.AluOpType.mult,
-                    op1=mybir.AluOpType.add,
-                )
+        def transposes(j, m):
+            words = g_sb[j][:].bitcast(F32).rearrange("p (o m) -> p o m", m=NPAIR)
+            xts[(j, m)] = psum.tile([P, PACK * P], F32, name="xt", tag="xt%d" % m)
+            for t in range(PACK):
+                nc.tensor.transpose(xts[(j, m)][:, t * P : (t + 1) * P], words[:, t * P : (t + 1) * P, m], ident[:])
 
-        def transposes(j):
-            words = g_sb[j][:].bitcast(F32).rearrange("p (o m) -> p o m", m=NPOS // 2)
-            sorted_words = g_sorted[j][:].bitcast(F32)
-            for m in range(NPOS // 2):
-                xts[(j, m)] = xt_pool.tile([P, PACK * P], F32, name="xt")
-                for t in range(PACK):
-                    if m < 2:
-                        in_ = words[:, t * P : (t + 1) * P, m]
-                    else:
-                        in_ = sorted_words[:, ((m - 2) * PACK + t) * P : ((m - 2) * PACK + t + 1) * P]
-                    nc.tensor.transpose(xts[(j, m)][:, t * P : (t + 1) * P], in_, ident[:])
-
-        def copies(j):
-            grouped[j] = grp_pool.tile([P, NPOS * P * PACK], BF16, name="grouped", align_bytes=64)
-            for m in range(NPOS // 2):
-                if m < 2:
-                    dst = grouped[j][:, m * 2 * P * PACK : (m + 1) * 2 * P * PACK].rearrange(
-                        "p (e b t) -> p e b t", e=2, t=PACK
-                    )
-                    src = xts[(j, m)][:].bitcast(BF16).rearrange("p (t b e) -> p e b t", t=PACK, e=2)
-                else:
-                    dst = grouped[j][:].bitcast(F32)[:, m * P * PACK : (m + 1) * P * PACK].rearrange(
-                        "p (n b u) -> p n b u", n=2, u=2
-                    )
-                    src = xts[(j, m)][:].rearrange("p (n u b) -> p n b u", n=2, u=2)
-                if m == 3:
-                    nc.vector.tensor_copy(out=dst, in_=src)
-                else:
-                    nc.scalar.copy(out=dst, in_=src)
+        def copy_g(j, m):
+            if m == 0:
+                grouped[j] = grp_pool.tile([P, NPOS * P * PACK], BF16, name="grouped", align_bytes=64)
+            dst = grouped[j][:, m * 2 * P * PACK : (m + 1) * 2 * P * PACK].rearrange(
+                "p (e b t) -> p e b t", e=2, t=PACK
+            )
+            src = xts[(j, m)][:].bitcast(BF16).rearrange("p (t b e) -> p e b t", t=PACK, e=2)
+            if m == 3 or (m == 1 and j in V_SECOND_BANK):
+                nc.vector.tensor_copy(out=dst, in_=src)
+            else:
+                nc.scalar.copy(out=dst, in_=src)
 
         def quantise_g(j):
             g_codes[j] = code_pool.tile([P, NPOS * P], U32, name="g_codes", align_bytes=64)
@@ -129,54 +107,79 @@ def tile_nonoverlappinglocallyconnected1d_t_kernel(tc, x, weight, grad_out, out)
                 in_=wg[:, n * COLS * PACK : (n + 1) * COLS * PACK],
             )
 
-        def product(j, n, o_sb):
-            acc = acc_pool.tile([P, COLS], F32, name="acc")
-            nc.tensor.matmul_mx(
-                out=acc[:],
-                lhsT=g_codes[j][:, n * P : (n + 1) * P].bitcast(E5M2X4),
-                lhsT_scale=g_scales[j][:, n * P : (n + 1) * P],
-                rhs=wc[:, n * COLS : (n + 1) * COLS].bitcast(E4M3X4),
-                rhs_scale=ws[:, n * COLS : (n + 1) * COLS],
-                start=True,
-                stop=True,
-            )
-            dst = o_sb[:].rearrange("p (i n k) -> p n i k", n=NPOS, k=BLK)[:, n]
-            src = acc[:].rearrange("p (i k) -> p i k", k=BLK)
-            on_scalar = n >= 4
-            if on_scalar:
-                nc.scalar.mul(out=dst, in_=src, mul=SCALE)
-            else:
-                nc.vector.tensor_scalar(out=dst, in0=src, scalar1=SCALE, scalar2=None, op0=mybir.AluOpType.mult)
+        def passes(j, m):
+            for n in (2 * m, 2 * m + 1):
+                kind = "xt" if (j == LAST and m >= 2) else "acc"
+                accs[(j, n)] = psum.tile([P, COLS], F32, name="acc", tag="%s%d" % (kind, n % 4))
+                nc.tensor.matmul_mx(
+                    out=accs[(j, n)][:],
+                    lhsT=g_codes[j][:, n * P : (n + 1) * P].bitcast(E5M2X4),
+                    lhsT_scale=g_scales[j][:, n * P : (n + 1) * P],
+                    rhs=wc[:, n * COLS : (n + 1) * COLS].bitcast(E4M3X4),
+                    rhs_scale=ws[:, n * COLS : (n + 1) * COLS],
+                    start=True,
+                    stop=True,
+                )
+
+        def copy_out(j, m, i0=0, i1=CIN):
+            if m == 0 and i0 == 0:
+                o_sb[j] = opool.tile([P, CIN * D], F32, name="o_sb")
+            for n in (2 * m, 2 * m + 1):
+                dst = o_sb[j][:].rearrange("p (i n k) -> p n i k", n=NPOS, k=BLK)[:, n, i0:i1]
+                src = accs[(j, n)][:].rearrange("p (i k) -> p i k", k=BLK)[:, i0:i1]
+                if m % 2 == 1:
+                    nc.scalar.mul(out=dst, in_=src, mul=SCALE)
+                else:
+                    nc.vector.tensor_scalar(out=dst, in0=src, scalar1=SCALE, scalar2=None, op0=mybir.AluOpType.mult)
 
         load_g(0)
         for c in range(WCH):
             load_w(c)
-        for j in range(1, 5):
+        for j in range(1, G_BUFS):
             load_g(j)
-        sort_g(0)
-        transposes(0)
-        copies(0)
-        load_g(5)
-        for c in range(WCH):
-            regroup_w(c)
-        quantise_g(0)
-        sort_g(1)
-        transposes(1)
-        copies(1)
-        load_g(6)
-        for j in range(NBT):
-            if j + 2 < NBT:
-                sort_g(j + 2)
-                transposes(j + 2)
-            if j == 0:
-                load_g(7)
-            o_sb = opool.tile([P, CIN * D], F32, name="o_sb")
-            for n in range(NPOS):
-                if j == 0:
+
+        for s in range(-2, LAST):
+            now = 0 <= s
+            ahead = s + 2 < NBT
+            if now:
+                passes(s, 0)
+                passes(s, 1)
+                copy_out(s, 0)
+                copy_out(s, 1)
+            if ahead:
+                transposes(s + 2, 0)
+                transposes(s + 2, 1)
+            if 0 < s + 1 < NBT:
+                quantise_g(s + 1)
+            if ahead:
+                copy_g(s + 2, 0)
+            if now:
+                passes(s, 2)
+                passes(s, 3)
+                copy_out(s, 2)
+                copy_out(s, 3)
+            if ahead:
+                transposes(s + 2, 2)
+                transposes(s + 2, 3)
+                if s + 2 + G_BUFS < NBT:
+                    load_g(s + 2 + G_BUFS)
+                copy_g(s + 2, 1)
+                copy_g(s + 2, 2)
+                copy_g(s + 2, 3)
+            if now:
+                nc.sync.dma_start(out=ov[s], in_=o_sb[s][:])
+            if s == -2:
+                regroup_w(0)
+                regroup_w(1)
+                quantise_g(0)
+                regroup_w(2)
+                regroup_w(3)
+                for n in range(NPOS):
                     quantise_w(n)
-                product(j, n, o_sb)
-            nc.sync.dma_start(out=ov[j], in_=o_sb[:])
-            if j + 1 < NBT:
-                quantise_g(j + 1)
-            if j + 2 < NBT:
-                copies(j + 2)
+
+        for m in range(NPAIR):
+            passes(LAST, m)
+        for i0 in (0, CIN // 2):
+            for m in range(NPAIR):
+                copy_out(LAST, m, i0, i0 + CIN // 2)
+            nc.sync.dma_start(out=ov[LAST][:, i0 * D : (i0 + CIN // 2) * D], in_=o_sb[LAST][:, i0 * D : (i0 + CIN // 2) * D])

@@ -26,8 +26,7 @@ SCALE = 1.0 / math.sqrt(CIN)
 FLOPS = 2 * NPOS * BS * COUT * COLS
 BYTES = 2 * COUT * CIN * D + 2 * BS * COUT * NPOS + 4 * BS * CIN * D
 
-V_NPOS = 6
-V_SECOND_BANK = (0, 4, 6)
+V_NPOS = 4
 LAST = NBT - 1
 
 
@@ -83,7 +82,7 @@ def tile_nonoverlappinglocallyconnected1d_t_kernel(tc, x, weight, grad_out, out)
                 "p (e b t) -> p e b t", e=2, t=PACK
             )
             src = xts[(j, m)][:].bitcast(BF16).rearrange("p (t b e) -> p e b t", t=PACK, e=2)
-            if m == 3 or (m == 1 and j in V_SECOND_BANK):
+            if m == 3 or (m == 1 and j % 2 == 0):
                 nc.vector.tensor_copy(out=dst, in_=src)
             else:
                 nc.scalar.copy(out=dst, in_=src)
@@ -100,12 +99,13 @@ def tile_nonoverlappinglocallyconnected1d_t_kernel(tc, x, weight, grad_out, out)
             for n in range(V_NPOS, NPOS):
                 nc.scalar.copy(out=dst[:, n], in_=src[:, n])
 
-        def quantise_w(n):
-            nc.vector.quantize_mx(
-                out=wc[:, n * COLS : (n + 1) * COLS].bitcast(E4M3X4),
-                scales=ws[:, n * COLS : (n + 1) * COLS],
-                in_=wg[:, n * COLS * PACK : (n + 1) * COLS * PACK],
-            )
+        def quantise_w(c, positions):
+            for n in positions:
+                lo = n * COLS + c * IC * BLK
+                hi = lo + IC * BLK
+                nc.vector.quantize_mx(
+                    out=wc[:, lo:hi].bitcast(E4M3X4), scales=ws[:, lo:hi], in_=wg[:, lo * PACK : hi * PACK]
+                )
 
         def passes(j, m):
             for n in (2 * m, 2 * m + 1):
@@ -169,13 +169,14 @@ def tile_nonoverlappinglocallyconnected1d_t_kernel(tc, x, weight, grad_out, out)
             if now:
                 nc.sync.dma_start(out=ov[s], in_=o_sb[s][:])
             if s == -2:
-                regroup_w(0)
-                regroup_w(1)
-                quantise_g(0)
-                regroup_w(2)
-                regroup_w(3)
-                for n in range(NPOS):
-                    quantise_w(n)
+                for c in range(WCH):
+                    regroup_w(c)
+                    if c > 0:
+                        quantise_w(c - 1, range(V_NPOS, NPOS))
+                    quantise_w(c, range(V_NPOS))
+                    if c == 1:
+                        quantise_g(0)
+                quantise_w(WCH - 1, range(V_NPOS, NPOS))
 
         for m in range(NPAIR):
             passes(LAST, m)

import math
from contextlib import ExitStack

import concourse.mybir as mybir
from concourse.masks import make_identity

BF16 = mybir.dt.bfloat16
F32 = mybir.dt.float32
U32 = mybir.dt.uint32
U8 = mybir.dt.uint8
E4M3X4 = mybir.dt.float8_e4m3fn_x4
E5M2X4 = mybir.dt.float8_e5m2_x4

P = 128
BS, CIN, COUT, NPOS, BLK = 1024, 128, 512, 8, 4
D = NPOS * BLK
PACK = 4
NBT = BS // P
NPAIR = NPOS // 2
COLS = CIN * BLK
WCH = 4
IC = CIN // WCH
G_BUFS = 6
SCALE = 1.0 / math.sqrt(CIN)

FLOPS = 2 * NPOS * BS * COUT * COLS
BYTES = 2 * COUT * CIN * D + 2 * BS * COUT * NPOS + 4 * BS * CIN * D

V_NPOS = 4
LAST = NBT - 1


def tile_nonoverlappinglocallyconnected1d_t_kernel(tc, x, weight, grad_out, out):
    nc = tc.nc
    gv = grad_out.rearrange("(j p) o n -> j p (o n)", p=P)
    ov = out.rearrange("(j p) i d -> j p (i d)", p=P)
    wv = weight.rearrange("(t p) i d -> p t (i d)", p=P)

    with ExitStack() as ctx:
        const = ctx.enter_context(tc.tile_pool(name="const", bufs=1))
        gpool = ctx.enter_context(tc.tile_pool(name="gpool", bufs=G_BUFS))
        wraw_pool = ctx.enter_context(tc.tile_pool(name="wraw", bufs=WCH))
        grp_pool = ctx.enter_context(tc.tile_pool(name="grp", bufs=2))
        code_pool = ctx.enter_context(tc.tile_pool(name="code", bufs=2))
        opool = ctx.enter_context(tc.tile_pool(name="opool", bufs=4))
        psum = ctx.enter_context(tc.psum_pool(name="psum", bufs=1))
        ctx.enter_context(tc.manual_schedule())

        ident = const.tile([P, P], F32)
        make_identity(nc, ident[:])
        wg = const.tile([P, NPOS * COLS * PACK], BF16, align_bytes=64)
        wc = const.tile([P, NPOS * COLS], U32, align_bytes=64)
        ws = const.tile([P, NPOS * COLS], U8, align_bytes=64)

        g_sb = {}
        xts = {}
        grouped = {}
        g_codes = {}
        g_scales = {}
        w_raw = {}
        accs = {}
        o_sb = {}

        def load_g(j):
            g_sb[j] = gpool.tile([P, COUT * NPOS], BF16, name="g_sb")
            nc.sync.dma_start(out=g_sb[j][:], in_=gv[j])

        def load_w(c):
            w_raw[c] = wraw_pool.tile([P, PACK, IC * D], BF16, name="w_raw")
            nc.sync.dma_start(out=w_raw[c][:], in_=wv[:, :, c * IC * D : (c + 1) * IC * D])

        def transposes(j, m):
            words = g_sb[j][:].bitcast(F32).rearrange("p (o m) -> p o m", m=NPAIR)
            xts[(j, m)] = psum.tile([P, PACK * P], F32, name="xt", tag="xt%d" % m)
            for t in range(PACK):
                nc.tensor.transpose(xts[(j, m)][:, t * P : (t + 1) * P], words[:, t * P : (t + 1) * P, m], ident[:])

        def copy_g(j, m):
            if m == 0:
                grouped[j] = grp_pool.tile([P, NPOS * P * PACK], BF16, name="grouped", align_bytes=64)
            dst = grouped[j][:, m * 2 * P * PACK : (m + 1) * 2 * P * PACK].rearrange(
                "p (e b t) -> p e b t", e=2, t=PACK
            )
            src = xts[(j, m)][:].bitcast(BF16).rearrange("p (t b e) -> p e b t", t=PACK, e=2)
            if m == 3 or (m == 1 and j % 2 == 0):
                nc.vector.tensor_copy(out=dst, in_=src)
            else:
                nc.scalar.copy(out=dst, in_=src)

        def quantise_g(j):
            g_codes[j] = code_pool.tile([P, NPOS * P], U32, name="g_codes", align_bytes=64)
            g_scales[j] = code_pool.tile([P, NPOS * P], U8, name="g_scales", align_bytes=64)
            nc.vector.quantize_mx(out=g_codes[j][:].bitcast(E5M2X4), scales=g_scales[j][:], in_=grouped[j][:])

        def regroup_w(c):
            src = w_raw[c][:].rearrange("p t (i n k) -> p n i t k", n=NPOS, k=BLK)
            dst = wg[:].rearrange("p (n i k t) -> p n i t k", n=NPOS, k=BLK, t=PACK)[:, :, c * IC : (c + 1) * IC]
            nc.vector.tensor_copy(out=dst[:, 0:V_NPOS], in_=src[:, 0:V_NPOS])
            for n in range(V_NPOS, NPOS):
                nc.scalar.copy(out=dst[:, n], in_=src[:, n])

        def quantise_w(c, positions):
            for n in positions:
                lo = n * COLS + c * IC * BLK
                hi = lo + IC * BLK
                nc.vector.quantize_mx(
                    out=wc[:, lo:hi].bitcast(E4M3X4), scales=ws[:, lo:hi], in_=wg[:, lo * PACK : hi * PACK]
                )

        def passes(j, m):
            for n in (2 * m, 2 * m + 1):
                kind = "xt" if (j == LAST and m >= 2) else "acc"
                accs[(j, n)] = psum.tile([P, COLS], F32, name="acc", tag="%s%d" % (kind, n % 4))
                nc.tensor.matmul_mx(
                    out=accs[(j, n)][:],
                    lhsT=g_codes[j][:, n * P : (n + 1) * P].bitcast(E5M2X4),
                    lhsT_scale=g_scales[j][:, n * P : (n + 1) * P],
                    rhs=wc[:, n * COLS : (n + 1) * COLS].bitcast(E4M3X4),
                    rhs_scale=ws[:, n * COLS : (n + 1) * COLS],
                    start=True,
                    stop=True,
                )

        def copy_out(j, m, i0=0, i1=CIN):
            if m == 0 and i0 == 0:
                o_sb[j] = opool.tile([P, CIN * D], F32, name="o_sb")
            for n in (2 * m, 2 * m + 1):
                dst = o_sb[j][:].rearrange("p (i n k) -> p n i k", n=NPOS, k=BLK)[:, n, i0:i1]
                src = accs[(j, n)][:].rearrange("p (i k) -> p i k", k=BLK)[:, i0:i1]
                if m % 2 == 1:
                    nc.scalar.mul(out=dst, in_=src, mul=SCALE)
                else:
                    nc.vector.tensor_scalar(out=dst, in0=src, scalar1=SCALE, scalar2=None, op0=mybir.AluOpType.mult)

        load_g(0)
        for c in range(WCH):
            load_w(c)
        for j in range(1, G_BUFS):
            load_g(j)

        for s in range(-2, LAST):
            now = 0 <= s
            ahead = s + 2 < NBT
            if now:
                passes(s, 0)
                passes(s, 1)
                copy_out(s, 0)
                copy_out(s, 1)
            if ahead:
                transposes(s + 2, 0)
                transposes(s + 2, 1)
            if 0 < s + 1 < NBT:
                quantise_g(s + 1)
            if ahead:
                copy_g(s + 2, 0)
            if now:
                passes(s, 2)
                passes(s, 3)
                copy_out(s, 2)
                copy_out(s, 3)
            if ahead:
                transposes(s + 2, 2)
                transposes(s + 2, 3)
                if s + 2 + G_BUFS < NBT:
                    load_g(s + 2 + G_BUFS)
                copy_g(s + 2, 1)
                copy_g(s + 2, 2)
                copy_g(s + 2, 3)
            if now:
                nc.sync.dma_start(out=ov[s], in_=o_sb[s][:])
            if s == -2:
                for c in range(WCH):
                    regroup_w(c)
                    if c > 0:
                        quantise_w(c - 1, range(V_NPOS, NPOS))
                    quantise_w(c, range(V_NPOS))
                    if c == 1:
                        quantise_g(0)
                quantise_w(WCH - 1, range(V_NPOS, NPOS))

        for m in range(NPAIR):
            passes(LAST, m)
        for i0 in (0, CIN // 2):
            for m in range(NPAIR):
                copy_out(LAST, m, i0, i0 + CIN // 2)
            nc.sync.dma_start(out=ov[LAST][:, i0 * D : (i0 + CIN // 2) * D], in_=o_sb[LAST][:, i0 * D : (i0 + CIN // 2) * D])
